import numpy as np
import ml_dtypes


BF16 = ml_dtypes.bfloat16


def bf(x):
    return np.asarray(x, np.float32).astype(BF16)


def f64(x):
    return np.asarray(x).astype(np.float64)


E2M1 = np.array([0.0, 0.5, 1.0, 1.5, 2.0, 3.0, 4.0, 6.0, -0.0, -0.5, -1.0, -1.5, -2.0, -3.0, -4.0, -6.0])


def pack_weight(w, fmt):
    k, n = w.shape
    w = f64(bf(w)).reshape(k // 32, 32, n)
    amax = np.abs(w).max(1)
    if fmt == "e4m3":
        byte = np.frexp(amax)[1] - 1 + 127 - 7
    else:
        mant, ex = np.frexp(amax / 6.0)
        byte = np.where(mant > 0.5, ex, ex - 1) + 127
    byte = np.clip(np.where(amax > 0, byte, 1), 1, 254)
    scaled = (w * np.exp2(127.0 - byte)[:, None, :]).reshape(k, n).astype(np.float32)
    by_word = np.ascontiguousarray(scaled.reshape(k // 512, 128, 4, n).transpose(0, 1, 3, 2))
    if fmt == "e4m3":
        words = by_word.astype(ml_dtypes.float8_e4m3fn).view(np.uint8)
    else:
        c = by_word.astype(ml_dtypes.float4_e2m1fn).view(np.uint8) & 0xF
        words = c[..., 0::2] | (c[..., 1::2] << 4)
    return np.ascontiguousarray(words), np.ascontiguousarray(byte.astype(np.uint8).reshape(k // 512, 16, n))


def unpack_weight(words, scales, fmt):
    g, p, n, _ = words.shape
    if fmt == "e4m3":
        vals = np.ascontiguousarray(words).view(ml_dtypes.float8_e4m3fn).astype(np.float64)
    else:
        nib = np.empty((g, p, n, 4), np.uint8)
        nib[..., 0::2] = words & 0xF
        nib[..., 1::2] = words >> 4
        vals = E2M1[nib]
    vals = vals * np.repeat(np.exp2(scales.astype(np.float64) - 127.0), 8, axis=1)[..., None]
    return vals.transpose(0, 1, 3, 2).reshape(g * 512, n)

def pack4(w):
    words, scales = pack_weight(w, "e2m1")
    return words.reshape(words.shape[0], 128, -1), scales


def unpack4(words, scales):
    return unpack_weight(words.reshape(words.shape[0], 128, -1, 2), scales, "e2m1")


def kspread(k):
    return np.exp2(np.repeat(np.random.randint(-6, 7, k // 32), 32).astype(np.float64))


B, S, D, H, QB = 1, 512, 1536, 8, 512
HD = D // H
HALF = HD // 2


def rope_cache():
    inv_freq = 1.0 / (10000.0 ** (np.arange(HALF) / max(HALF, 1)))
    ang = np.arange(S)[:, None] * inv_freq[None, :]
    return np.cos(ang)[None, None], np.sin(ang)[None, None]


def apply_rope(u, cos, sin):
    u1, u2 = u[..., :HALF], u[..., HALF:]
    return np.concatenate([u1 * cos - u2 * sin, u1 * sin + u2 * cos], axis=-1)


def setup_inputs():
    s = kspread(D)
    x = np.random.standard_normal((B, S, D)) * s
    Wq = np.random.standard_normal((2 * D, D)) / np.sqrt(D) / s[None, :]
    bq = bf(np.random.standard_normal(2 * D) * 0.2)
    Wk = np.random.standard_normal((2 * D, D)) / np.sqrt(D) / s[None, :]
    bk = bf(np.random.standard_normal(2 * D) * 0.2)
    x_words, x_scales = pack4(np.ascontiguousarray(x.reshape(B * S, D).T))
    Wq_words, Wq_scales = pack4(np.ascontiguousarray(Wq.T))
    Wk_words, Wk_scales = pack4(np.ascontiguousarray(Wk.T))
    return {"x_words": x_words, "x_scales": x_scales,
            "Wq_words": Wq_words, "Wq_scales": Wq_scales,
            "bq": bq,
            "Wk_words": Wk_words, "Wk_scales": Wk_scales,
            "bk": bk}


def reference(x_words, x_scales, Wq_words, Wq_scales, bq, Wk_words, Wk_scales, bk):
    xq = unpack4(x_words, x_scales).T.reshape(B, S, D)
    q = ((xq @ unpack4(Wq_words, Wq_scales)) + f64(bq)).reshape(B, S, H, 2 * HD).transpose(0, 2, 1, 3)
    k = ((xq @ unpack4(Wk_words, Wk_scales)) + f64(bk)).reshape(B, S, H, 2 * HD).transpose(0, 2, 1, 3)
    cos, sin = rope_cache()
    q1, q2 = apply_rope(q[..., :HD], cos, sin), apply_rope(q[..., HD:], cos, sin)
    k1, k2 = apply_rope(k[..., :HD], cos, sin), apply_rope(k[..., HD:], cos, sin)
    return q1, q2, k1, k2

@@ -1,0 +1,214 @@
+import math
+from contextlib import ExitStack
+
+import concourse.mybir as mybir
+from concourse.masks import make_identity
+
+P = 128
+K = 1536
+TOKENS = 512
+CHANNELS = 3072
+HEADS = 8
+SUB = 192
+HALF = 96
+HEAD_CH = 2 * SUB
+PASSES = K // 512
+TB = TOKENS // P
+TILES_PER_HEAD = HEAD_CH // P
+
+FLOPS = 2 * TOKENS * K * 2 * CHANNELS
+
+F32 = mybir.dt.float32
+BF16 = mybir.dt.bfloat16
+I32 = mybir.dt.int32
+U8 = mybir.dt.uint8
+FP4X4 = mybir.dt.float4_e2m1fn_x4
+ADD = mybir.AluOpType.add
+MULT = mybir.AluOpType.mult
+SUBTRACT = mybir.AluOpType.subtract
+ACT = mybir.ActivationFunctionType
+
+
+def tile_differentialselfattention_pa_kernel(
+    tc, x_words, x_scales, wq_words, wq_scales, bq, wk_words, wk_scales, bk, out_0, out_1, out_2, out_3
+):
+    nc = tc.nc
+    with ExitStack() as ctx:
+        keep = ctx.enter_context(tc.tile_pool(name="keep", bufs=1))
+        work = ctx.enter_context(tc.tile_pool(name="work", bufs=3))
+        psum_acc = ctx.enter_context(tc.psum_pool(name="psum_acc", bufs=3))
+        psum_tok = ctx.enter_context(tc.psum_pool(name="psum_tok", bufs=5))
+        ctx.enter_context(tc.manual_schedule())
+
+        x_codes = keep.tile([P, PASSES, 2 * TOKENS], U8, name="x_codes", align_bytes=64)
+        x_planes = keep.tile([P, PASSES, TOKENS], U8, name="x_planes", align_bytes=64)
+        chunks = []
+        for first, count in ((0, 1), (1, 1), (2, 2), (4, 4), (8, 8)):
+            codes = keep.tile([P, PASSES, 2 * count * HEAD_CH], U8, name=f"codes{first}", align_bytes=64)
+            planes = keep.tile([P, PASSES, count * HEAD_CH], U8, name=f"planes{first}", align_bytes=64)
+            chunks.append((first, count, codes, planes))
+
+        def flat32(tile):
+            return tile[:].rearrange("p g n -> p (g n)").bitcast(I32)
+
+        pos = keep.tile([P, TB], F32, name="pos")
+        nc.gpsimd.iota(pos[:], pattern=[[1, TB]], base=0, channel_multiplier=TB, allow_small_or_imprecise_dtypes=True)
+        bias_rows = keep.tile([P, P], BF16, name="bias_rows")
+        nc.gpsimd.memset(bias_rows[:], 0.0)
+        rows = CHANNELS // P
+        nc.gpsimd.dma_start(out=bias_rows[0:rows, :], in_=bq.rearrange("(t c) -> t c", c=P))
+        nc.gpsimd.dma_start(out=bias_rows[rows : 2 * rows, :], in_=bk.rearrange("(t c) -> t c", c=P))
+        ident = keep.tile([P, P], F32, name="ident")
+        make_identity(nc, ident[:])
+        for _, _, _, planes in chunks[1:]:
+            nc.gpsimd.memset(flat32(planes), 0)
+
+        nc.vector.memset(flat32(x_planes), 0)
+        nc.vector.memset(flat32(chunks[0][3]), 0)
+
+        def load_codes(dst, src, lo, hi):
+            nc.sync.dma_start(
+                out=dst[:].bitcast(I32), in_=src[:, :, 2 * lo : 2 * hi].rearrange("g p n -> p g n").bitcast(I32)
+            )
+
+        def load_scales(dst, src, lo, hi):
+            for quad in range(4):
+                nc.sync.dma_start(
+                    out=dst[32 * quad : 32 * quad + 4, :, :].bitcast(I32),
+                    in_=src[:, 4 * quad : 4 * quad + 4, lo:hi].rearrange("g r n -> r g n").bitcast(I32),
+                )
+
+        def chunk_source(first, count):
+            words, scales = (wq_words, wq_scales) if first < HEADS else (wk_words, wk_scales)
+            lo = (first % HEADS) * HEAD_CH
+            return words, scales, lo, lo + count * HEAD_CH
+
+        load_codes(x_codes, x_words, 0, TOKENS)
+        words, scales, lo, hi = chunk_source(chunks[0][0], chunks[0][1])
+        load_codes(chunks[0][2], words, lo, hi)
+        load_scales(x_planes, x_scales, 0, TOKENS)
+        load_scales(chunks[0][3], scales, lo, hi)
+        for first, count, codes, planes in chunks[1:]:
+            words, scales, lo, hi = chunk_source(first, count)
+            load_codes(codes, words, lo, hi)
+            load_scales(planes, scales, lo, hi)
+
+        freq = keep.tile([P, HALF], F32, name="freq")
+        ratio = 10000.0 ** (-1.0 / HALF)
+        nc.vector.memset(freq[:, 0:1], 1.0)
+        width = 1
+        while width < HALF:
+            count = min(width, HALF - width)
+            nc.vector.tensor_scalar(
+                out=freq[:, width : width + count], in0=freq[:, 0:count], scalar1=ratio**width, scalar2=None, op0=MULT
+            )
+            width += count
+        turns = keep.tile([P, 2, TB, HALF], F32, name="turns")
+        for tb in range(TB):
+            nc.vector.tensor_scalar(
+                out=turns[:, 0, tb, :], in0=freq[:], scalar1=pos[:, tb : tb + 1], scalar2=1.0 / (2.0 * math.pi), op0=MULT, op1=MULT
+            )
+        nc.vector.tensor_scalar(out=turns[:, 1], in0=turns[:, 0], scalar1=0.25, scalar2=None, op0=ADD)
+        whole = keep.tile([P, 2, TB, HALF], I32, name="whole")
+        nc.vector.tensor_copy(out=whole[:], in_=turns[:])
+        frac = keep.tile([P, 2, TB, HALF], F32, name="frac")
+        nc.vector.tensor_tensor(out=frac[:], in0=turns[:], in1=whole[:], op=SUBTRACT)
+
+        warm = keep.tile([P, 1], F32, name="warm")
+        nc.vector.memset(warm[:], 0.0)
+        warm_out = keep.tile([P, 1], F32, name="warm_out")
+        nc.scalar.activation(out=warm_out[:], in_=warm[:], func=ACT.Sin)
+
+        bias_f32 = keep.tile([P, P], F32, name="bias_f32")
+        nc.scalar.copy(out=bias_f32[:], in_=bias_rows[:])
+        bias_ps = psum_acc.tile([P, TOKENS], F32, name="acc")
+        nc.tensor.transpose(bias_ps[:, 0:P], bias_f32[:], ident[:])
+        bias_cols = keep.tile([P, 2 * rows], F32, name="bias_cols")
+        nc.scalar.copy(out=bias_cols[:], in_=bias_ps[:, 0 : 2 * rows])
+
+        cos_t = keep.tile([P, TB, 1, HALF], F32, name="cos_t")
+        sin_t = keep.tile([P, TB, 2, HALF], F32, name="sin_t")
+        nc.scalar.activation(out=cos_t[:, :, 0, :], in_=frac[:, 1], func=ACT.Sin, scale=2.0 * math.pi)
+        nc.scalar.activation(out=sin_t[:, :, 0, :], in_=frac[:, 0], func=ACT.Sin, scale=-2.0 * math.pi)
+        nc.scalar.activation(out=sin_t[:, :, 1, :], in_=frac[:, 0], func=ACT.Sin, scale=2.0 * math.pi)
+
+        w_tiles = {}
+
+        def project(n):
+            h, j = divmod(n, TILES_PER_HEAD)
+            for first, count, codes, planes in chunks:
+                if first <= h < first + count:
+                    break
+            col = (h - first) * HEAD_CH + j * P
+            acc = psum_acc.tile([P, TOKENS], F32, name="acc")
+            for g in range(PASSES):
+                nc.tensor.matmul_mx(
+                    out=acc[:],
+                    lhsT=codes[:, g, 2 * col : 2 * (col + P)].bitcast(FP4X4),
+                    lhsT_scale=planes[:, g, col : col + P],
+                    rhs=x_codes[:, g, :].bitcast(FP4X4),
+                    rhs_scale=x_planes[:, g, :],
+                    start=(g == 0),
+                    stop=(g == PASSES - 1),
+                )
+            if j == 0:
+                w_new = work.tile([P, TILES_PER_HEAD, TB, P], F32, name="w_new")
+                w_tiles[h] = w_new
+            nc.scalar.activation(
+                out=w_tiles[h][:, j],
+                in_=acc[:].rearrange("c (p t) -> c t p", t=TB),
+                func=ACT.Identity,
+                bias=bias_cols[:, n : n + 1],
+                scale=1.0,
+            )
+
+        def rotate(h):
+            w_head = w_tiles[h]
+            p_cos = work.tile([P, TB, 2, SUB], F32, name="p_cos")
+            p_sin = work.tile([P, TB, 2, SUB], F32, name="p_sin")
+            for tb in range(TB):
+                tok = psum_tok.tile([P, HEAD_CH], F32, name="tok")
+                for j in range(TILES_PER_HEAD):
+                    nc.tensor.transpose(tok[:, j * P : (j + 1) * P], w_head[:, j, tb, :], ident[:])
+                nc.vector.tensor_tensor(
+                    out=p_cos[:, tb].rearrange("p s (h i) -> p (s h) i", i=HALF),
+                    in0=tok[:].rearrange("p (a i) -> p a i", i=HALF),
+                    in1=cos_t[:, tb].to_broadcast([P, 4, HALF]),
+                    op=MULT,
+                )
+                nc.vector.tensor_tensor(
+                    out=p_sin[:, tb].rearrange("p s (h i) -> p s h i", i=HALF),
+                    in0=tok[:].rearrange("p (s h i) -> p s h i", h=2, i=HALF)[:, :, ::-1, :],
+                    in1=sin_t[:, tb : tb + 1].to_broadcast([P, 2, 2, HALF]),
+                    op=MULT,
+                )
+            r = work.tile([P, 2, TB, SUB], F32, name="r")
+            outs = (out_0, out_1) if h < HEADS else (out_2, out_3)
+            dsts = [o[0, h % HEADS].rearrange("(p t) n -> p t n", t=TB) for o in outs]
+            if h == 2 * HEADS - 1:
+                for lo, hi in ((0, 1), (1, 2), (2, 3), (3, 4)):
+                    nc.gpsimd.tensor_tensor(
+                        out=r[:, :, lo:hi, :],
+                        in0=p_cos[:, lo:hi].rearrange("p t s n -> p s t n"),
+                        in1=p_sin[:, lo:hi].rearrange("p t s n -> p s t n"),
+                        op=ADD,
+                    )
+                for lo, hi in ((0, 2), (2, 3), (3, 4)):
+                    for s in range(2):
+                        nc.sync.dma_start(out=dsts[s][:, lo:hi, :], in_=r[:, s, lo:hi, :])
+                return
+            nc.gpsimd.tensor_tensor(
+                out=r[:],
+                in0=p_cos[:].rearrange("p t s n -> p s t n"),
+                in1=p_sin[:].rearrange("p t s n -> p s t n"),
+                op=ADD,
+            )
+            for s in range(2):
+                nc.sync.dma_start(out=dsts[s], in_=r[:, s])
+
+        tiles = 2 * HEADS * TILES_PER_HEAD
+        for n in range(tiles):
+            project(n)
+            if n % TILES_PER_HEAD == 0 and n > 0:
+                rotate(n // TILES_PER_HEAD - 1)
+        rotate(2 * HEADS - 1)

@@ -63,16 +63,20 @@ def tile_differentialselfattention_pa_kernel(
         for _, _, _, planes in chunks[1:]:
             nc.gpsimd.memset(flat32(planes), 0)
 
+        warm = keep.tile([P, 1], F32, name="warm")
+        nc.vector.memset(warm[:], 0.0)
         nc.vector.memset(flat32(x_planes), 0)
         nc.vector.memset(flat32(chunks[0][3]), 0)
+        zeros = keep.tile([P, TOKENS], BF16, name="zeros")
+        nc.vector.memset(zeros[:], 0.0)
 
         def load_codes(dst, src, lo, hi):
             nc.sync.dma_start(
                 out=dst[:].bitcast(I32), in_=src[:, :, 2 * lo : 2 * hi].rearrange("g p n -> p g n").bitcast(I32)
             )
 
-        def load_scales(dst, src, lo, hi):
-            for quad in range(4):
+        def load_scales(dst, src, lo, hi, quads=range(4)):
+            for quad in quads:
                 nc.sync.dma_start(
                     out=dst[32 * quad : 32 * quad + 4, :, :].bitcast(I32),
                     in_=src[:, 4 * quad : 4 * quad + 4, lo:hi].rearrange("g r n -> r g n").bitcast(I32),
@@ -83,10 +87,11 @@ def tile_differentialselfattention_pa_kernel(
             lo = (first % HEADS) * HEAD_CH
             return words, scales, lo, lo + count * HEAD_CH
 
-        load_codes(x_codes, x_words, 0, TOKENS)
         words, scales, lo, hi = chunk_source(chunks[0][0], chunks[0][1])
+        load_scales(x_planes, x_scales, 0, TOKENS, (0, 1))
         load_codes(chunks[0][2], words, lo, hi)
-        load_scales(x_planes, x_scales, 0, TOKENS)
+        load_codes(x_codes, x_words, 0, TOKENS)
+        load_scales(x_planes, x_scales, 0, TOKENS, (2, 3))
         load_scales(chunks[0][3], scales, lo, hi)
         for first, count, codes, planes in chunks[1:]:
             words, scales, lo, hi = chunk_source(first, count)
@@ -114,13 +119,14 @@ def tile_differentialselfattention_pa_kernel(
         frac = keep.tile([P, 2, TB, HALF], F32, name="frac")
         nc.vector.tensor_tensor(out=frac[:], in0=turns[:], in1=whole[:], op=SUBTRACT)
 
-        warm = keep.tile([P, 1], F32, name="warm")
-        nc.vector.memset(warm[:], 0.0)
         warm_out = keep.tile([P, 1], F32, name="warm_out")
         nc.scalar.activation(out=warm_out[:], in_=warm[:], func=ACT.Sin)
 
         bias_f32 = keep.tile([P, P], F32, name="bias_f32")
         nc.scalar.copy(out=bias_f32[:], in_=bias_rows[:])
+        for _ in range(12):
+            dummy = psum_tok.tile([P, TOKENS], F32, name="tok")
+            nc.tensor.matmul(dummy[:], zeros[:, 0:P], zeros[:], start=True, stop=True)
         bias_ps = psum_acc.tile([P, TOKENS], F32, name="acc")
         nc.tensor.transpose(bias_ps[:, 0:P], bias_f32[:], ident[:])
         bias_cols = keep.tile([P, 2 * rows], F32, name="bias_cols")
@@ -167,44 +173,35 @@ def tile_differentialselfattention_pa_kernel(
             p_cos = work.tile([P, TB, 2, SUB], F32, name="p_cos")
             p_sin = work.tile([P, TB, 2, SUB], F32, name="p_sin")
             for tb in range(TB):
-                tok = psum_tok.tile([P, HEAD_CH], F32, name="tok")
+                tok = psum_tok.tile([P, TOKENS], F32, name="tok")
                 for j in range(TILES_PER_HEAD):
                     nc.tensor.transpose(tok[:, j * P : (j + 1) * P], w_head[:, j, tb, :], ident[:])
                 nc.vector.tensor_tensor(
                     out=p_cos[:, tb].rearrange("p s (h i) -> p (s h) i", i=HALF),
-                    in0=tok[:].rearrange("p (a i) -> p a i", i=HALF),
+                    in0=tok[:, 0:HEAD_CH].rearrange("p (a i) -> p a i", i=HALF),
                     in1=cos_t[:, tb].to_broadcast([P, 4, HALF]),
                     op=MULT,
                 )
                 nc.vector.tensor_tensor(
                     out=p_sin[:, tb].rearrange("p s (h i) -> p s h i", i=HALF),
-                    in0=tok[:].rearrange("p (s h i) -> p s h i", h=2, i=HALF)[:, :, ::-1, :],
+                    in0=tok[:, 0:HEAD_CH].rearrange("p (s h i) -> p s h i", h=2, i=HALF)[:, :, ::-1, :],
                     in1=sin_t[:, tb : tb + 1].to_broadcast([P, 2, 2, HALF]),
                     op=MULT,
                 )
             r = work.tile([P, 2, TB, SUB], F32, name="r")
             outs = (out_0, out_1) if h < HEADS else (out_2, out_3)
             dsts = [o[0, h % HEADS].rearrange("(p t) n -> p t n", t=TB) for o in outs]
-            if h == 2 * HEADS - 1:
-                for lo, hi in ((0, 1), (1, 2), (2, 3), (3, 4)):
-                    nc.gpsimd.tensor_tensor(
-                        out=r[:, :, lo:hi, :],
-                        in0=p_cos[:, lo:hi].rearrange("p t s n -> p s t n"),
-                        in1=p_sin[:, lo:hi].rearrange("p t s n -> p s t n"),
-                        op=ADD,
-                    )
-                for lo, hi in ((0, 2), (2, 3), (3, 4)):
-                    for s in range(2):
-                        nc.sync.dma_start(out=dsts[s][:, lo:hi, :], in_=r[:, s, lo:hi, :])
-                return
-            nc.gpsimd.tensor_tensor(
-                out=r[:],
-                in0=p_cos[:].rearrange("p t s n -> p s t n"),
-                in1=p_sin[:].rearrange("p t s n -> p s t n"),
-                op=ADD,
-            )
-            for s in range(2):
-                nc.sync.dma_start(out=dsts[s], in_=r[:, s])
+            last = h == 2 * HEADS - 1
+            for lo, hi in ((0, 2), (2, 4)) if not last else ((0, 2), (2, 3), (3, 4)):
+                nc.gpsimd.tensor_tensor(
+                    out=r[:, :, lo:hi, :],
+                    in0=p_cos[:, lo:hi].rearrange("p t s n -> p s t n"),
+                    in1=p_sin[:, lo:hi].rearrange("p t s n -> p s t n"),
+                    op=ADD,
+                )
+            for lo, hi in ((0, 4),) if not last else ((0, 2), (2, 3), (3, 4)):
+                for s in range(2):
+                    nc.sync.dma_start(out=dsts[s][:, lo:hi, :], in_=r[:, s, lo:hi, :])
 
         tiles = 2 * HEADS * TILES_PER_HEAD
         for n in range(tiles):

@@ -35,17 +35,17 @@ def tile_differentialselfattention_pa_kernel(
     nc = tc.nc
     with ExitStack() as ctx:
         keep = ctx.enter_context(tc.tile_pool(name="keep", bufs=1))
-        work = ctx.enter_context(tc.tile_pool(name="work", bufs=3))
+        work = ctx.enter_context(tc.tile_pool(name="work", bufs=4))
         psum_acc = ctx.enter_context(tc.psum_pool(name="psum_acc", bufs=3))
         psum_tok = ctx.enter_context(tc.psum_pool(name="psum_tok", bufs=5))
         ctx.enter_context(tc.manual_schedule())
 
-        x_codes = keep.tile([P, PASSES, 2 * TOKENS], U8, name="x_codes", align_bytes=64)
-        x_planes = keep.tile([P, PASSES, TOKENS], U8, name="x_planes", align_bytes=64)
+        x_codes = keep.tile([P, PASSES, 2 * TOKENS], U8, name="x_codes", align_bytes=256)
+        x_planes = keep.tile([P, PASSES, TOKENS], U8, name="x_planes", align_bytes=256)
         chunks = []
         for first, count in ((0, 1), (1, 1), (2, 2), (4, 4), (8, 8)):
-            codes = keep.tile([P, PASSES, 2 * count * HEAD_CH], U8, name=f"codes{first}", align_bytes=64)
-            planes = keep.tile([P, PASSES, count * HEAD_CH], U8, name=f"planes{first}", align_bytes=64)
+            codes = keep.tile([P, PASSES, 2 * count * HEAD_CH], U8, name=f"codes{first}", align_bytes=256)
+            planes = keep.tile([P, PASSES, count * HEAD_CH], U8, name=f"planes{first}", align_bytes=256)
             chunks.append((first, count, codes, planes))
 
         def flat32(tile):
@@ -170,20 +170,20 @@ def tile_differentialselfattention_pa_kernel(
 
         def rotate(h):
             w_head = w_tiles[h]
-            p_cos = work.tile([P, TB, 2, SUB], F32, name="p_cos")
-            p_sin = work.tile([P, TB, 2, SUB], F32, name="p_sin")
+            p_cos = work.tile([P, 2, TB, SUB], F32, name="p_cos")
+            p_sin = work.tile([P, 2, TB, SUB], F32, name="p_sin")
             for tb in range(TB):
                 tok = psum_tok.tile([P, TOKENS], F32, name="tok")
                 for j in range(TILES_PER_HEAD):
                     nc.tensor.transpose(tok[:, j * P : (j + 1) * P], w_head[:, j, tb, :], ident[:])
                 nc.vector.tensor_tensor(
-                    out=p_cos[:, tb].rearrange("p s (h i) -> p (s h) i", i=HALF),
-                    in0=tok[:, 0:HEAD_CH].rearrange("p (a i) -> p a i", i=HALF),
-                    in1=cos_t[:, tb].to_broadcast([P, 4, HALF]),
+                    out=p_cos[:, :, tb].rearrange("p s (h i) -> p s h i", i=HALF),
+                    in0=tok[:, 0:HEAD_CH].rearrange("p (s h i) -> p s h i", h=2, i=HALF),
+                    in1=cos_t[:, tb : tb + 1].to_broadcast([P, 2, 2, HALF]),
                     op=MULT,
                 )
                 nc.vector.tensor_tensor(
-                    out=p_sin[:, tb].rearrange("p s (h i) -> p s h i", i=HALF),
+                    out=p_sin[:, :, tb].rearrange("p s (h i) -> p s h i", i=HALF),
                     in0=tok[:, 0:HEAD_CH].rearrange("p (s h i) -> p s h i", h=2, i=HALF)[:, :, ::-1, :],
                     in1=sin_t[:, tb : tb + 1].to_broadcast([P, 2, 2, HALF]),
                     op=MULT,
@@ -192,11 +192,17 @@ def tile_differentialselfattention_pa_kernel(
             outs = (out_0, out_1) if h < HEADS else (out_2, out_3)
             dsts = [o[0, h % HEADS].rearrange("(p t) n -> p t n", t=TB) for o in outs]
             last = h == 2 * HEADS - 1
-            for lo, hi in ((0, 2), (2, 4)) if not last else ((0, 2), (2, 3), (3, 4)):
+            if last:
+                cuts = ((0, 2), (2, 3), (3, 4))
+            elif h in (0, 2 * HEADS - 3, 2 * HEADS - 2):
+                cuts = ((0, 2), (2, 4))
+            else:
+                cuts = ((0, 4),)
+            for lo, hi in cuts:
                 nc.gpsimd.tensor_tensor(
                     out=r[:, :, lo:hi, :],
-                    in0=p_cos[:, lo:hi].rearrange("p t s n -> p s t n"),
-                    in1=p_sin[:, lo:hi].rearrange("p t s n -> p s t n"),
+                    in0=p_cos[:, :, lo:hi, :],
+                    in1=p_sin[:, :, lo:hi, :],
                     op=ADD,
                 )
             for lo, hi in ((0, 4),) if not last else ((0, 2), (2, 3), (3, 4)):

@@ -52,23 +52,20 @@ def tile_differentialselfattention_pa_kernel(
             return tile[:].rearrange("p g n -> p (g n)").bitcast(I32)
 
         pos = keep.tile([P, TB], F32, name="pos")
-        nc.gpsimd.iota(pos[:], pattern=[[1, TB]], base=0, channel_multiplier=TB, allow_small_or_imprecise_dtypes=True)
         bias_rows = keep.tile([P, P], BF16, name="bias_rows")
-        nc.gpsimd.memset(bias_rows[:], 0.0)
         rows = CHANNELS // P
-        nc.gpsimd.dma_start(out=bias_rows[0:rows, :], in_=bq.rearrange("(t c) -> t c", c=P))
-        nc.gpsimd.dma_start(out=bias_rows[rows : 2 * rows, :], in_=bk.rearrange("(t c) -> t c", c=P))
+        nc.gpsimd.memset(bias_rows[:].bitcast(I32), 0)
+        nc.gpsimd.memset(flat32(x_planes), 0)
+        nc.gpsimd.iota(pos[:], pattern=[[1, TB]], base=0, channel_multiplier=TB, allow_small_or_imprecise_dtypes=True)
         ident = keep.tile([P, P], F32, name="ident")
         make_identity(nc, ident[:])
-        for _, _, _, planes in chunks[1:]:
-            nc.gpsimd.memset(flat32(planes), 0)
+        nc.gpsimd.memset(flat32(chunks[1][3]), 0)
 
         warm = keep.tile([P, 1], F32, name="warm")
         nc.vector.memset(warm[:], 0.0)
-        nc.vector.memset(flat32(x_planes), 0)
         nc.vector.memset(flat32(chunks[0][3]), 0)
         zeros = keep.tile([P, TOKENS], BF16, name="zeros")
-        nc.vector.memset(zeros[:], 0.0)
+        nc.vector.memset(zeros[:].bitcast(I32), 0)
 
         def load_codes(dst, src, lo, hi):
             nc.sync.dma_start(
@@ -88,55 +85,69 @@ def tile_differentialselfattention_pa_kernel(
             return words, scales, lo, lo + count * HEAD_CH
 
         words, scales, lo, hi = chunk_source(chunks[0][0], chunks[0][1])
+        nc.sync.dma_start(out=bias_rows[0:rows, :], in_=bq.rearrange("(t c) -> t c", c=P))
+        nc.sync.dma_start(out=bias_rows[rows : 2 * rows, :], in_=bk.rearrange("(t c) -> t c", c=P))
         load_scales(x_planes, x_scales, 0, TOKENS, (0, 1))
         load_codes(chunks[0][2], words, lo, hi)
         load_codes(x_codes, x_words, 0, TOKENS)
         load_scales(x_planes, x_scales, 0, TOKENS, (2, 3))
         load_scales(chunks[0][3], scales, lo, hi)
-        for first, count, codes, planes in chunks[1:]:
-            words, scales, lo, hi = chunk_source(first, count)
-            load_codes(codes, words, lo, hi)
-            load_scales(planes, scales, lo, hi)
-
-        freq = keep.tile([P, HALF], F32, name="freq")
         ratio = 10000.0 ** (-1.0 / HALF)
-        nc.vector.memset(freq[:, 0:1], 1.0)
+        turns = keep.tile([P, TB, HALF], F32, name="turns")
+        nc.vector.tensor_scalar(out=turns[:, :, 0], in0=pos[:], scalar1=1.0 / (2.0 * math.pi), scalar2=None, op0=MULT)
         width = 1
         while width < HALF:
             count = min(width, HALF - width)
             nc.vector.tensor_scalar(
-                out=freq[:, width : width + count], in0=freq[:, 0:count], scalar1=ratio**width, scalar2=None, op0=MULT
+                out=turns[:, :, width : width + count],
+                in0=turns[:, :, 0:count],
+                scalar1=ratio**width,
+                scalar2=None,
+                op0=MULT,
             )
             width += count
-        turns = keep.tile([P, 2, TB, HALF], F32, name="turns")
-        for tb in range(TB):
-            nc.vector.tensor_scalar(
-                out=turns[:, 0, tb, :], in0=freq[:], scalar1=pos[:, tb : tb + 1], scalar2=1.0 / (2.0 * math.pi), op0=MULT, op1=MULT
-            )
-        nc.vector.tensor_scalar(out=turns[:, 1], in0=turns[:, 0], scalar1=0.25, scalar2=None, op0=ADD)
-        whole = keep.tile([P, 2, TB, HALF], I32, name="whole")
-        nc.vector.tensor_copy(out=whole[:], in_=turns[:])
-        frac = keep.tile([P, 2, TB, HALF], F32, name="frac")
-        nc.vector.tensor_tensor(out=frac[:], in0=turns[:], in1=whole[:], op=SUBTRACT)
+        whole_sin = keep.tile([P, TB, HALF], I32, name="whole_sin")
+        whole_cos = keep.tile([P, TB, HALF], I32, name="whole_cos")
+        frac_sin = keep.tile([P, TB, HALF], F32, name="frac_sin")
+        frac_cos = keep.tile([P, TB, HALF], F32, name="frac_cos")
+        nc.vector.tensor_scalar(out=whole_cos[:], in0=turns[:], scalar1=0.25, scalar2=None, op0=ADD)
+        nc.vector.tensor_copy(out=whole_sin[:], in_=turns[:])
+        nc.vector.scalar_tensor_tensor(
+            out=frac_cos[:], in0=turns[:], scalar=0.25, in1=whole_cos[:], op0=ADD, op1=SUBTRACT
+        )
+        nc.vector.tensor_tensor(out=frac_sin[:], in0=turns[:], in1=whole_sin[:], op=SUBTRACT)
+        order = keep.tile([P, 1], F32, name="order")
+        nc.gpsimd.tensor_copy(out=order[:], in_=frac_sin[:, 0, 0:1])
+        for _, _, _, planes in chunks[2:]:
+            nc.gpsimd.memset(flat32(planes), 0)
+
+        for first, count, codes, planes in chunks[1:]:
+            words, scales, lo, hi = chunk_source(first, count)
+            load_codes(codes, words, lo, hi)
+            load_scales(planes, scales, lo, hi)
 
         warm_out = keep.tile([P, 1], F32, name="warm_out")
         nc.scalar.activation(out=warm_out[:], in_=warm[:], func=ACT.Sin)
 
         bias_f32 = keep.tile([P, P], F32, name="bias_f32")
         nc.scalar.copy(out=bias_f32[:], in_=bias_rows[:])
-        for _ in range(12):
-            dummy = psum_tok.tile([P, TOKENS], F32, name="tok")
-            nc.tensor.matmul(dummy[:], zeros[:, 0:P], zeros[:], start=True, stop=True)
+        def spin(count):
+            for _ in range(count):
+                dummy = psum_tok.tile([P, TOKENS], F32, name="tok")
+                nc.tensor.matmul(dummy[:], zeros[:, 0:P], zeros[:], start=True, stop=True)
+
+        spin(6)
         bias_ps = psum_acc.tile([P, TOKENS], F32, name="acc")
         nc.tensor.transpose(bias_ps[:, 0:P], bias_f32[:], ident[:])
         bias_cols = keep.tile([P, 2 * rows], F32, name="bias_cols")
         nc.scalar.copy(out=bias_cols[:], in_=bias_ps[:, 0 : 2 * rows])
+        spin(6)
 
         cos_t = keep.tile([P, TB, 1, HALF], F32, name="cos_t")
         sin_t = keep.tile([P, TB, 2, HALF], F32, name="sin_t")
-        nc.scalar.activation(out=cos_t[:, :, 0, :], in_=frac[:, 1], func=ACT.Sin, scale=2.0 * math.pi)
-        nc.scalar.activation(out=sin_t[:, :, 0, :], in_=frac[:, 0], func=ACT.Sin, scale=-2.0 * math.pi)
-        nc.scalar.activation(out=sin_t[:, :, 1, :], in_=frac[:, 0], func=ACT.Sin, scale=2.0 * math.pi)
+        nc.scalar.activation(out=cos_t[:, :, 0, :], in_=frac_cos[:], func=ACT.Sin, scale=2.0 * math.pi)
+        nc.scalar.activation(out=sin_t[:, :, 0, :], in_=frac_sin[:], func=ACT.Sin, scale=-2.0 * math.pi)
+        nc.scalar.activation(out=sin_t[:, :, 1, :], in_=frac_sin[:], func=ACT.Sin, scale=2.0 * math.pi)
 
         w_tiles = {}
 
@@ -192,20 +203,19 @@ def tile_differentialselfattention_pa_kernel(
             outs = (out_0, out_1) if h < HEADS else (out_2, out_3)
             dsts = [o[0, h % HEADS].rearrange("(p t) n -> p t n", t=TB) for o in outs]
             last = h == 2 * HEADS - 1
-            if last:
-                cuts = ((0, 2), (2, 3), (3, 4))
-            elif h in (0, 2 * HEADS - 3, 2 * HEADS - 2):
+            if last or h in (0, 2 * HEADS - 2):
                 cuts = ((0, 2), (2, 4))
             else:
                 cuts = ((0, 4),)
             for lo, hi in cuts:
-                nc.gpsimd.tensor_tensor(
+                adder = nc.vector if last else nc.gpsimd
+                adder.tensor_tensor(
                     out=r[:, :, lo:hi, :],
                     in0=p_cos[:, :, lo:hi, :],
                     in1=p_sin[:, :, lo:hi, :],
                     op=ADD,
                 )
-            for lo, hi in ((0, 4),) if not last else ((0, 2), (2, 3), (3, 4)):
+            for lo, hi in ((0, 4),) if not last else ((0, 2), (2, 4)):
                 for s in range(2):
                     nc.sync.dma_start(out=dsts[s][:, lo:hi, :], in_=r[:, s, lo:hi, :])
 

import math
from contextlib import ExitStack

import concourse.mybir as mybir
from concourse.masks import make_identity

P = 128
K = 1536
TOKENS = 512
CHANNELS = 3072
HEADS = 8
SUB = 192
HALF = 96
HEAD_CH = 2 * SUB
PASSES = K // 512
TB = TOKENS // P
TILES_PER_HEAD = HEAD_CH // P

FLOPS = 2 * TOKENS * K * 2 * CHANNELS

F32 = mybir.dt.float32
BF16 = mybir.dt.bfloat16
I32 = mybir.dt.int32
U8 = mybir.dt.uint8
FP4X4 = mybir.dt.float4_e2m1fn_x4
ADD = mybir.AluOpType.add
MULT = mybir.AluOpType.mult
SUBTRACT = mybir.AluOpType.subtract
ACT = mybir.ActivationFunctionType


def tile_differentialselfattention_pa_kernel(
    tc, x_words, x_scales, wq_words, wq_scales, bq, wk_words, wk_scales, bk, out_0, out_1, out_2, out_3
):
    nc = tc.nc
    with ExitStack() as ctx:
        keep = ctx.enter_context(tc.tile_pool(name="keep", bufs=1))
        work = ctx.enter_context(tc.tile_pool(name="work", bufs=4))
        psum_acc = ctx.enter_context(tc.psum_pool(name="psum_acc", bufs=3))
        psum_tok = ctx.enter_context(tc.psum_pool(name="psum_tok", bufs=5))
        ctx.enter_context(tc.manual_schedule())

        x_codes = keep.tile([P, PASSES, 2 * TOKENS], U8, name="x_codes", align_bytes=256)
        x_planes = keep.tile([P, PASSES, TOKENS], U8, name="x_planes", align_bytes=256)
        chunks = []
        for first, count in ((0, 1), (1, 1), (2, 2), (4, 4), (8, 8)):
            codes = keep.tile([P, PASSES, 2 * count * HEAD_CH], U8, name=f"codes{first}", align_bytes=256)
            planes = keep.tile([P, PASSES, count * HEAD_CH], U8, name=f"planes{first}", align_bytes=256)
            chunks.append((first, count, codes, planes))

        def flat32(tile):
            return tile[:].rearrange("p g n -> p (g n)").bitcast(I32)

        pos = keep.tile([P, TB], F32, name="pos")
        bias_rows = keep.tile([P, P], BF16, name="bias_rows")
        rows = CHANNELS // P
        nc.gpsimd.memset(bias_rows[:].bitcast(I32), 0)
        nc.gpsimd.memset(flat32(x_planes), 0)
        nc.gpsimd.iota(pos[:], pattern=[[1, TB]], base=0, channel_multiplier=TB, allow_small_or_imprecise_dtypes=True)
        ident = keep.tile([P, P], F32, name="ident")
        make_identity(nc, ident[:])
        nc.gpsimd.memset(flat32(chunks[1][3]), 0)

        warm = keep.tile([P, 1], F32, name="warm")
        nc.vector.memset(warm[:], 0.0)
        nc.vector.memset(flat32(chunks[0][3]), 0)
        zeros = keep.tile([P, TOKENS], BF16, name="zeros")
        nc.vector.memset(zeros[:].bitcast(I32), 0)

        def load_codes(dst, src, lo, hi):
            nc.sync.dma_start(
                out=dst[:].bitcast(I32), in_=src[:, :, 2 * lo : 2 * hi].rearrange("g p n -> p g n").bitcast(I32)
            )

        def load_scales(dst, src, lo, hi, quads=range(4)):
            for quad in quads:
                nc.sync.dma_start(
                    out=dst[32 * quad : 32 * quad + 4, :, :].bitcast(I32),
                    in_=src[:, 4 * quad : 4 * quad + 4, lo:hi].rearrange("g r n -> r g n").bitcast(I32),
                )

        def chunk_source(first, count):
            words, scales = (wq_words, wq_scales) if first < HEADS else (wk_words, wk_scales)
            lo = (first % HEADS) * HEAD_CH
            return words, scales, lo, lo + count * HEAD_CH

        words, scales, lo, hi = chunk_source(chunks[0][0], chunks[0][1])
        nc.sync.dma_start(out=bias_rows[0:rows, :], in_=bq.rearrange("(t c) -> t c", c=P))
        nc.sync.dma_start(out=bias_rows[rows : 2 * rows, :], in_=bk.rearrange("(t c) -> t c", c=P))
        load_scales(x_planes, x_scales, 0, TOKENS, (0, 1))
        load_codes(chunks[0][2], words, lo, hi)
        load_codes(x_codes, x_words, 0, TOKENS)
        load_scales(x_planes, x_scales, 0, TOKENS, (2, 3))
        load_scales(chunks[0][3], scales, lo, hi)
        ratio = 10000.0 ** (-1.0 / HALF)
        turns = keep.tile([P, TB, HALF], F32, name="turns")
        nc.vector.tensor_scalar(out=turns[:, :, 0], in0=pos[:], scalar1=1.0 / (2.0 * math.pi), scalar2=None, op0=MULT)
        width = 1
        while width < HALF:
            count = min(width, HALF - width)
            nc.vector.tensor_scalar(
                out=turns[:, :, width : width + count],
                in0=turns[:, :, 0:count],
                scalar1=ratio**width,
                scalar2=None,
                op0=MULT,
            )
            width += count
        whole_sin = keep.tile([P, TB, HALF], I32, name="whole_sin")
        whole_cos = keep.tile([P, TB, HALF], I32, name="whole_cos")
        frac_sin = keep.tile([P, TB, HALF], F32, name="frac_sin")
        frac_cos = keep.tile([P, TB, HALF], F32, name="frac_cos")
        nc.vector.tensor_scalar(out=whole_cos[:], in0=turns[:], scalar1=0.25, scalar2=None, op0=ADD)
        nc.vector.tensor_copy(out=whole_sin[:], in_=turns[:])
        nc.vector.scalar_tensor_tensor(
            out=frac_cos[:], in0=turns[:], scalar=0.25, in1=whole_cos[:], op0=ADD, op1=SUBTRACT
        )
        nc.vector.tensor_tensor(out=frac_sin[:], in0=turns[:], in1=whole_sin[:], op=SUBTRACT)
        order = keep.tile([P, 1], F32, name="order")
        nc.gpsimd.tensor_copy(out=order[:], in_=frac_sin[:, 0, 0:1])
        for _, _, _, planes in chunks[2:]:
            nc.gpsimd.memset(flat32(planes), 0)

        for first, count, codes, planes in chunks[1:]:
            words, scales, lo, hi = chunk_source(first, count)
            load_codes(codes, words, lo, hi)
            load_scales(planes, scales, lo, hi)

        warm_out = keep.tile([P, 1], F32, name="warm_out")
        nc.scalar.activation(out=warm_out[:], in_=warm[:], func=ACT.Sin)

        bias_f32 = keep.tile([P, P], F32, name="bias_f32")
        nc.scalar.copy(out=bias_f32[:], in_=bias_rows[:])
        def spin(count):
            for _ in range(count):
                dummy = psum_tok.tile([P, TOKENS], F32, name="tok")
                nc.tensor.matmul(dummy[:], zeros[:, 0:P], zeros[:], start=True, stop=True)

        spin(6)
        bias_ps = psum_acc.tile([P, TOKENS], F32, name="acc")
        nc.tensor.transpose(bias_ps[:, 0:P], bias_f32[:], ident[:])
        bias_cols = keep.tile([P, 2 * rows], F32, name="bias_cols")
        nc.scalar.copy(out=bias_cols[:], in_=bias_ps[:, 0 : 2 * rows])
        spin(6)

        cos_t = keep.tile([P, TB, 1, HALF], F32, name="cos_t")
        sin_t = keep.tile([P, TB, 2, HALF], F32, name="sin_t")
        nc.scalar.activation(out=cos_t[:, :, 0, :], in_=frac_cos[:], func=ACT.Sin, scale=2.0 * math.pi)
        nc.scalar.activation(out=sin_t[:, :, 0, :], in_=frac_sin[:], func=ACT.Sin, scale=-2.0 * math.pi)
        nc.scalar.activation(out=sin_t[:, :, 1, :], in_=frac_sin[:], func=ACT.Sin, scale=2.0 * math.pi)

        w_tiles = {}

        def project(n):
            h, j = divmod(n, TILES_PER_HEAD)
            for first, count, codes, planes in chunks:
                if first <= h < first + count:
                    break
            col = (h - first) * HEAD_CH + j * P
            acc = psum_acc.tile([P, TOKENS], F32, name="acc")
            for g in range(PASSES):
                nc.tensor.matmul_mx(
                    out=acc[:],
                    lhsT=codes[:, g, 2 * col : 2 * (col + P)].bitcast(FP4X4),
                    lhsT_scale=planes[:, g, col : col + P],
                    rhs=x_codes[:, g, :].bitcast(FP4X4),
                    rhs_scale=x_planes[:, g, :],
                    start=(g == 0),
                    stop=(g == PASSES - 1),
                )
            if j == 0:
                w_new = work.tile([P, TILES_PER_HEAD, TB, P], F32, name="w_new")
                w_tiles[h] = w_new
            nc.scalar.activation(
                out=w_tiles[h][:, j],
                in_=acc[:].rearrange("c (p t) -> c t p", t=TB),
                func=ACT.Identity,
                bias=bias_cols[:, n : n + 1],
                scale=1.0,
            )

        def rotate(h):
            w_head = w_tiles[h]
            p_cos = work.tile([P, 2, TB, SUB], F32, name="p_cos")
            p_sin = work.tile([P, 2, TB, SUB], F32, name="p_sin")
            for tb in range(TB):
                tok = psum_tok.tile([P, TOKENS], F32, name="tok")
                for j in range(TILES_PER_HEAD):
                    nc.tensor.transpose(tok[:, j * P : (j + 1) * P], w_head[:, j, tb, :], ident[:])
                nc.vector.tensor_tensor(
                    out=p_cos[:, :, tb].rearrange("p s (h i) -> p s h i", i=HALF),
                    in0=tok[:, 0:HEAD_CH].rearrange("p (s h i) -> p s h i", h=2, i=HALF),
                    in1=cos_t[:, tb : tb + 1].to_broadcast([P, 2, 2, HALF]),
                    op=MULT,
                )
                nc.vector.tensor_tensor(
                    out=p_sin[:, :, tb].rearrange("p s (h i) -> p s h i", i=HALF),
                    in0=tok[:, 0:HEAD_CH].rearrange("p (s h i) -> p s h i", h=2, i=HALF)[:, :, ::-1, :],
                    in1=sin_t[:, tb : tb + 1].to_broadcast([P, 2, 2, HALF]),
                    op=MULT,
                )
            r = work.tile([P, 2, TB, SUB], F32, name="r")
            outs = (out_0, out_1) if h < HEADS else (out_2, out_3)
            dsts = [o[0, h % HEADS].rearrange("(p t) n -> p t n", t=TB) for o in outs]
            last = h == 2 * HEADS - 1
            if last or h in (0, 2 * HEADS - 2):
                cuts = ((0, 2), (2, 4))
            else:
                cuts = ((0, 4),)
            for lo, hi in cuts:
                adder = nc.vector if last else nc.gpsimd
                adder.tensor_tensor(
                    out=r[:, :, lo:hi, :],
                    in0=p_cos[:, :, lo:hi, :],
                    in1=p_sin[:, :, lo:hi, :],
                    op=ADD,
                )
            for lo, hi in ((0, 4),) if not last else ((0, 2), (2, 4)):
                for s in range(2):
                    nc.sync.dma_start(out=dsts[s][:, lo:hi, :], in_=r[:, s, lo:hi, :])

        tiles = 2 * HEADS * TILES_PER_HEAD
        for n in range(tiles):
            project(n)
            if n % TILES_PER_HEAD == 0 and n > 0:
                rotate(n // TILES_PER_HEAD - 1)
        rotate(2 * HEADS - 1)
